import numpy as np
import ml_dtypes


def mxq(x, axis, fmt="e4m3"):
    dtype, down = {"e4m3": (ml_dtypes.float8_e4m3fn, 7), "e5m2": (ml_dtypes.float8_e5m2, 14)}[fmt]
    v = np.moveaxis(np.asarray(x, np.float32).astype(ml_dtypes.bfloat16).astype(np.float64), axis, -1)
    blocks = v.reshape(v.shape[:-1] + (-1, 32))
    amax = np.abs(blocks).max(-1, keepdims=True)
    byte = np.maximum(np.where(amax > 0, np.frexp(amax)[1] - 1 + 127, 0) - down, 1)
    scale = np.exp2(byte - 127.0)
    codes = (blocks / scale).astype(np.float32).astype(dtype).astype(np.float64)
    return np.moveaxis((codes * scale).reshape(v.shape), -1, axis)


WIDE = False


def mx_kscale(k):
    if not WIDE:
        return np.ones(k)
    levels = np.array([10, -10, 5, -5, 0])
    a = np.random.permutation(np.resize(levels, k // 512 * 4)).reshape(k // 512, 4)
    idx = np.arange(k)
    return np.exp2(a[idx // 512, idx % 128 // 32])


BF16 = ml_dtypes.bfloat16


def bf(x):
    return np.asarray(x, np.float32).astype(BF16)


def f64(x):
    return np.asarray(x).astype(np.float64)


B, T, C, H, KH, D = 4, 128, 2048, 16, 4, 128
HD = H * D


def sigmoid(v):
    return 1.0 / (1.0 + np.exp(-v))


def setup_inputs():
    s, t = mx_kscale(C), mx_kscale(HD)
    return {"x": bf(np.random.standard_normal((B, T, C)) * s),
            "y_attn": bf((np.random.standard_normal((B, T, HD)) * 0.3 * t).reshape(B, T, H, D)),
            "w_gate": bf(np.random.standard_normal((C, HD)) / np.sqrt(C) / s[:, None]),
            "w_proj": bf(np.random.standard_normal((HD, C)) * 3.0 / np.sqrt(HD) / t[:, None])}


def reference(x, y_attn, w_gate, w_proj):
    gate = sigmoid((mxq(f64(x), 2, "e4m3") @ mxq(f64(w_gate), 0, "e4m3")).reshape(B, T, H, D))
    y = f64(y_attn) * gate
    return mxq(y.reshape(B, T, HD), 2, "e4m3") @ mxq(f64(w_proj), 0, "e4m3")

@@ -1,0 +1,256 @@
+from contextlib import ExitStack
+
+import concourse.bass as bass
+import concourse.mybir as mybir
+import concourse.tile as tile
+from concourse.masks import make_identity
+
+F32 = mybir.dt.float32
+BF16 = mybir.dt.bfloat16
+U32 = mybir.dt.uint32
+U8 = mybir.dt.uint8
+FP8X4 = mybir.dt.float8_e4m3fn_x4
+ACT = mybir.ActivationFunctionType
+ALU = mybir.AluOpType
+
+P = 128
+M = 512
+C = 2048
+NG = 4
+CH = 512
+NCH = C // CH
+MT = M // P
+
+FLOPS = 2 * 2 * M * C * C
+
+NB_RAW = 18
+V_SHARE_1 = 7
+V_SHARE_2 = 10
+
+
+def on_vector(i, share):
+    return ((i + 1) * share) // 16 - (i * share) // 16 == 1
+
+
+def tile_multiheadattention_pb_kernel(tc, x, y_attn, w_gate, w_proj, out):
+    nc = tc.nc
+    xf = x.flatten_outer_dims()
+    yf = y_attn.rearrange("b t h d -> (b t) (h d)")
+    of = out.flatten_outer_dims()
+
+    with ExitStack() as ctx:
+        const = ctx.enter_context(tc.tile_pool(name="const", bufs=1))
+        keep = ctx.enter_context(tc.tile_pool(name="keep", bufs=1))
+        rawp = ctx.enter_context(tc.tile_pool(name="rawp", bufs=NB_RAW))
+        grpp = ctx.enter_context(tc.tile_pool(name="grpp", bufs=6))
+        xgp = ctx.enter_context(tc.tile_pool(name="xgp", bufs=4))
+        wcp = ctx.enter_context(tc.tile_pool(name="wcp", bufs=3))
+        sigp = ctx.enter_context(tc.tile_pool(name="sigp", bufs=3))
+        hgp = ctx.enter_context(tc.tile_pool(name="hgp", bufs=2))
+        outp = ctx.enter_context(tc.tile_pool(name="outp", bufs=8))
+        psum = ctx.enter_context(tc.psum_pool(name="psum", bufs=6))
+        psy = ctx.enter_context(tc.psum_pool(name="psy", bufs=2))
+
+        ident_f = const.tile([P, P], F32, name="ident_f")
+        make_identity(nc, ident_f[:])
+        ident_b = const.tile([P, P], BF16, name="ident_b")
+        make_identity(nc, ident_b[:])
+
+        x_sb = [keep.tile([P, C], BF16, name="x_sb%d" % mt) for mt in range(MT)]
+        y_sb = [keep.tile([P, MT, CH], BF16, name="y_sb%d" % c) for c in range(NCH)]
+        xc = keep.tile([P, NG, M], U32, name="xc", align_bytes=64)
+        xs = keep.tile([P, NG, M], U8, name="xs", align_bytes=64)
+        hc = keep.tile([P, NG, M], U32, name="hc", align_bytes=64)
+        hs = keep.tile([P, NG, M], U8, name="hs", align_bytes=64)
+
+        raws = {}
+
+        def load_x(mt):
+            nc.sync.dma_start(out=x_sb[mt][:], in_=xf[P * mt:P * (mt + 1), :])
+
+        def load_y(c):
+            nc.sync.dma_start(
+                out=y_sb[c][:],
+                in_=yf[:, CH * c:CH * (c + 1)].rearrange("(t p) c -> p t c", p=P),
+            )
+
+        def load_unit(i):
+            raw = rawp.tile([P, 4, CH], BF16, name="raw")
+            raws[i] = raw
+            c, g = (i % 16) // NG, i % NG
+            cols = slice(CH * c, CH * (c + 1))
+            if i < 16:
+                for u in range(2):
+                    r0 = 512 * g + 256 * u
+                    nc.sync.dma_start(
+                        out=raw[:, 2 * u:2 * u + 2, :],
+                        in_=w_gate[r0:r0 + 256, cols].rearrange("(q e) c -> q e c", e=2),
+                    )
+            else:
+                nc.sync.dma_start(
+                    out=raw[:],
+                    in_=w_proj[512 * g:512 * (g + 1), cols].rearrange("(j p) c -> p j c", p=P),
+                )
+
+        load_unit(0)
+        load_x(0)
+        load_x(1)
+        load_unit(1)
+        load_x(2)
+        load_x(3)
+        load_unit(2)
+        load_unit(3)
+        load_y(0)
+        for i in range(4, NB_RAW):
+            if i % 4 == 0 and i < 16:
+                load_y(i // 4)
+            load_unit(i)
+
+        wcs = {}
+        grps = {}
+
+        def regroup(i):
+            c, g = (i % 16) // NG, i % NG
+            grp = grpp.tile([P, 4 * CH], BF16, name="grp", align_bytes=64)
+            grps[i] = grp
+            dst = grp[:].rearrange("p (c i t) -> p c t i", i=4, t=4)
+            src = raws[i][:].rearrange("p t (c i) -> p c t i", i=4)
+            if on_vector(i % 16, V_SHARE_1 if i < 16 else V_SHARE_2):
+                nc.vector.tensor_copy(out=dst, in_=src)
+            else:
+                nc.scalar.copy(out=dst, in_=src)
+            if i + NB_RAW < 32:
+                load_unit(i + NB_RAW)
+
+        def quantise(i):
+            g = i % NG
+            if g == 0:
+                wcod = wcp.tile([P, NG, CH], U32, name="wcod", align_bytes=64)
+                wsca = wcp.tile([P, NG, CH], U8, name="wsca", align_bytes=64)
+                wcs[i // NG] = (wcod, wsca)
+            wcod, wsca = wcs[i // NG]
+            nc.vector.quantize_mx(
+                out=wcod[:, g, :].bitcast(FP8X4), scales=wsca[:, g, :], in_=grps[i][:]
+            )
+
+        def x_stage(half):
+            for g in range(NG):
+                ps = psum.tile([P, 2, 256], F32, name="bank")
+                for u in range(2):
+                    for i in range(2):
+                        w0 = 256 * g + 128 * u
+                        nc.tensor.transpose(
+                            ps[:, u, P * i:P * (i + 1)],
+                            x_sb[2 * half + i][:].bitcast(F32)[:, w0:w0 + P],
+                            ident_f[:],
+                        )
+                xg = xgp.tile([P, 1024], BF16, name="xg", align_bytes=64)
+                dst = xg[:].bitcast(F32).rearrange("p (m u) -> p m u", u=2)
+                src = ps[:].rearrange("p u m -> p m u")
+                if g % 2 == 0:
+                    nc.scalar.copy(out=dst, in_=src)
+                else:
+                    nc.vector.tensor_copy(out=dst, in_=src)
+                nc.vector.quantize_mx(
+                    out=xc[:, g, 256 * half:256 * (half + 1)].bitcast(FP8X4),
+                    scales=xs[:, g, 256 * half:256 * (half + 1)],
+                    in_=xg[:],
+                )
+
+        def phase1(c):
+            wcod, wsca = wcs[c]
+            yps = []
+            for half in range(2):
+                yp = psy.tile([P, 4, 256], BF16, name="ybank")
+                yps.append(yp)
+                for j in range(4):
+                    for i in range(2):
+                        nc.tensor.transpose(
+                            yp[:, j, P * i:P * (i + 1)],
+                            y_sb[c][:, 2 * half + i, P * j:P * (j + 1)],
+                            ident_b[:],
+                        )
+            hg = hgp.tile([P, 4 * M], BF16, name="hg", align_bytes=64)
+            for half in range(2):
+                sig = sigp.tile([P, 1024], F32, name="sig")
+                for i in range(2):
+                    mt = 2 * half + i
+                    acc = psum.tile([P, 4, P], F32, name="bank")
+                    for j in range(4):
+                        for g in range(NG):
+                            nc.tensor.matmul_mx(
+                                out=acc[:, j, :],
+                                lhsT=wcod[:, g, P * j:P * (j + 1)].bitcast(FP8X4),
+                                lhsT_scale=wsca[:, g, P * j:P * (j + 1)],
+                                rhs=xc[:, g, P * mt:P * (mt + 1)].bitcast(FP8X4),
+                                rhs_scale=xs[:, g, P * mt:P * (mt + 1)],
+                                start=(g == 0),
+                                stop=(g == NG - 1),
+                            )
+                    nc.scalar.activation(
+                        out=sig[:, 512 * i:512 * (i + 1)].rearrange("p (m j) -> p m j", j=4),
+                        in_=acc[:].rearrange("p j m -> p m j"),
+                        func=ACT.Sigmoid,
+                    )
+                nc.vector.tensor_tensor(
+                    out=hg[:, 1024 * half:1024 * (half + 1)].rearrange("p (m j) -> p m j", j=4),
+                    in0=sig[:].rearrange("p (m j) -> p m j", j=4),
+                    in1=yps[half][:].rearrange("p j m -> p m j"),
+                    op=ALU.mult,
+                )
+            nc.vector.quantize_mx(
+                out=hc[:, c, :].bitcast(FP8X4), scales=hs[:, c, :], in_=hg[:]
+            )
+
+        def phase2_pass(c, accs, g):
+            wcod, wsca = wcs[4 + c]
+            for mt in range(MT):
+                nc.tensor.matmul_mx(
+                    out=accs[mt][:],
+                    lhsT=hc[:, g, P * mt:P * (mt + 1)].bitcast(FP8X4),
+                    lhsT_scale=hs[:, g, P * mt:P * (mt + 1)],
+                    rhs=wcod[:, g, :].bitcast(FP8X4),
+                    rhs_scale=wsca[:, g, :],
+                    start=(g == 0),
+                    stop=(g == NG - 1),
+                )
+
+        def phase2_out(c, accs):
+            for mt in range(MT):
+                ob = outp.tile([P, CH], F32, name="ob")
+                if mt % 2 == 0:
+                    nc.scalar.copy(out=ob[:], in_=accs[mt][:])
+                else:
+                    nc.vector.tensor_copy(out=ob[:], in_=accs[mt][:])
+                nc.sync.dma_start(
+                    out=of[P * mt:P * (mt + 1), CH * c:CH * (c + 1)], in_=ob[:]
+                )
+
+        regroup(0)
+        x_stage(0)
+        regroup(1)
+        quantise(0)
+        x_stage(1)
+        regroup(2)
+        quantise(1)
+        regroup(3)
+        quantise(2)
+        quantise(3)
+        for c in range(NCH):
+            if c + 1 < NCH:
+                for g in range(NG):
+                    regroup(4 * (c + 1) + g)
+                    if g > 0:
+                        quantise(4 * (c + 1) + g - 1)
+                quantise(4 * (c + 1) + 3)
+            phase1(c)
+        for c in range(NCH):
+            accs = [psum.tile([P, CH], F32, name="bank") for mt in range(MT)]
+            for g in range(NG):
+                regroup(16 + 4 * c + g)
+                if g > 0:
+                    quantise(16 + 4 * c + g - 1)
+                    phase2_pass(c, accs, g - 1)
+            quantise(16 + 4 * c + 3)
+            phase2_pass(c, accs, 3)
+            phase2_out(c, accs)

@@ -1,8 +1,6 @@
 from contextlib import ExitStack
 
-import concourse.bass as bass
 import concourse.mybir as mybir
-import concourse.tile as tile
 from concourse.masks import make_identity
 
 F32 = mybir.dt.float32
@@ -17,19 +15,21 @@ P = 128
 M = 512
 C = 2048
 NG = 4
+LW = 1024
 CH = 512
-NCH = C // CH
 MT = M // P
 
 FLOPS = 2 * 2 * M * C * C
 
-NB_RAW = 18
-V_SHARE_1 = 7
-V_SHARE_2 = 10
-
-
-def on_vector(i, share):
-    return ((i + 1) * share) // 16 - (i * share) // 16 == 1
+NB_RAW = 9
+S_BOTH = ()
+LAG_S = (0, 1)
+LAG_V = (1, 2)
+ORDER2 = ("k", "c")
+V_BOTH = ()
+LAG_E = 2
+V_EVAC = (2, 3)
+Y_AFTER = (4, 8)
 
 
 def tile_multiheadattention_pb_kernel(tc, x, y_attn, w_gate, w_proj, out):
@@ -44,12 +44,13 @@ def tile_multiheadattention_pb_kernel(tc, x, y_attn, w_gate, w_proj, out):
         rawp = ctx.enter_context(tc.tile_pool(name="rawp", bufs=NB_RAW))
         grpp = ctx.enter_context(tc.tile_pool(name="grpp", bufs=6))
         xgp = ctx.enter_context(tc.tile_pool(name="xgp", bufs=4))
-        wcp = ctx.enter_context(tc.tile_pool(name="wcp", bufs=3))
+        wcp = ctx.enter_context(tc.tile_pool(name="wcp", bufs=8))
         sigp = ctx.enter_context(tc.tile_pool(name="sigp", bufs=3))
         hgp = ctx.enter_context(tc.tile_pool(name="hgp", bufs=2))
         outp = ctx.enter_context(tc.tile_pool(name="outp", bufs=8))
-        psum = ctx.enter_context(tc.psum_pool(name="psum", bufs=6))
-        psy = ctx.enter_context(tc.psum_pool(name="psy", bufs=2))
+        psum = ctx.enter_context(tc.psum_pool(name="psum", bufs=8))
+
+        ctx.enter_context(tc.manual_schedule())
 
         ident_f = const.tile([P, P], F32, name="ident_f")
         make_identity(nc, ident_f[:])
@@ -57,7 +58,7 @@ def tile_multiheadattention_pb_kernel(tc, x, y_attn, w_gate, w_proj, out):
         make_identity(nc, ident_b[:])
 
         x_sb = [keep.tile([P, C], BF16, name="x_sb%d" % mt) for mt in range(MT)]
-        y_sb = [keep.tile([P, MT, CH], BF16, name="y_sb%d" % c) for c in range(NCH)]
+        y_sb = [keep.tile([P, MT, LW], BF16, name="y_sb%d" % r) for r in range(2)]
         xc = keep.tile([P, NG, M], U32, name="xc", align_bytes=64)
         xs = keep.tile([P, NG, M], U8, name="xs", align_bytes=64)
         hc = keep.tile([P, NG, M], U32, name="hc", align_bytes=64)
@@ -68,18 +69,18 @@ def tile_multiheadattention_pb_kernel(tc, x, y_attn, w_gate, w_proj, out):
         def load_x(mt):
             nc.sync.dma_start(out=x_sb[mt][:], in_=xf[P * mt:P * (mt + 1), :])
 
-        def load_y(c):
+        def load_y(r):
             nc.sync.dma_start(
-                out=y_sb[c][:],
-                in_=yf[:, CH * c:CH * (c + 1)].rearrange("(t p) c -> p t c", p=P),
+                out=y_sb[r][:],
+                in_=yf[:, LW * r:LW * (r + 1)].rearrange("(t p) c -> p t c", p=P),
             )
 
         def load_unit(i):
-            raw = rawp.tile([P, 4, CH], BF16, name="raw")
+            raw = rawp.tile([P, 4, LW], BF16, name="raw")
             raws[i] = raw
-            c, g = (i % 16) // NG, i % NG
-            cols = slice(CH * c, CH * (c + 1))
-            if i < 16:
+            r, g = (i // NG) % 2, i % NG
+            cols = slice(LW * r, LW * (r + 1))
+            if i < 8:
                 for u in range(2):
                     r0 = 512 * g + 256 * u
                     nc.sync.dma_start(
@@ -93,47 +94,39 @@ def tile_multiheadattention_pb_kernel(tc, x, y_attn, w_gate, w_proj, out):
                 )
 
         load_unit(0)
-        load_x(0)
-        load_x(1)
-        load_unit(1)
-        load_x(2)
-        load_x(3)
-        load_unit(2)
-        load_unit(3)
-        load_y(0)
-        for i in range(4, NB_RAW):
-            if i % 4 == 0 and i < 16:
-                load_y(i // 4)
+        for mt in range(MT):
+            load_x(mt)
+        for i in range(1, NB_RAW):
             load_unit(i)
+            if i in Y_AFTER:
+                load_y(Y_AFTER.index(i))
 
-        wcs = {}
         grps = {}
+        cods = {}
+        done_units = {}
 
-        def regroup(i):
-            c, g = (i % 16) // NG, i % NG
+        def regroup(n, eng):
+            i, h = n // 2, n % 2
             grp = grpp.tile([P, 4 * CH], BF16, name="grp", align_bytes=64)
-            grps[i] = grp
+            grps[n] = grp
             dst = grp[:].rearrange("p (c i t) -> p c t i", i=4, t=4)
-            src = raws[i][:].rearrange("p t (c i) -> p c t i", i=4)
-            if on_vector(i % 16, V_SHARE_1 if i < 16 else V_SHARE_2):
+            src = raws[i][:, :, CH * h:CH * (h + 1)].rearrange("p t (c i) -> p c t i", i=4)
+            if eng == "v":
                 nc.vector.tensor_copy(out=dst, in_=src)
             else:
                 nc.scalar.copy(out=dst, in_=src)
-            if i + NB_RAW < 32:
+            done_units[i] = done_units.get(i, 0) + 1
+            if done_units[i] == 2 and i + NB_RAW < 16:
                 load_unit(i + NB_RAW)
 
-        def quantise(i):
-            g = i % NG
-            if g == 0:
-                wcod = wcp.tile([P, NG, CH], U32, name="wcod", align_bytes=64)
-                wsca = wcp.tile([P, NG, CH], U8, name="wsca", align_bytes=64)
-                wcs[i // NG] = (wcod, wsca)
-            wcod, wsca = wcs[i // NG]
-            nc.vector.quantize_mx(
-                out=wcod[:, g, :].bitcast(FP8X4), scales=wsca[:, g, :], in_=grps[i][:]
-            )
+        def quantise(n):
+            wcod = wcp.tile([P, CH], U32, name="wcod", align_bytes=64)
+            wsca = wcp.tile([P, CH], U8, name="wsca", align_bytes=64)
+            cods[n] = (wcod, wsca)
+            nc.vector.quantize_mx(out=wcod[:].bitcast(FP8X4), scales=wsca[:], in_=grps[n][:])
 
         def x_stage(half):
+            xgs = []
             for g in range(NG):
                 ps = psum.tile([P, 2, 256], F32, name="bank")
                 for u in range(2):
@@ -145,112 +138,176 @@ def tile_multiheadattention_pb_kernel(tc, x, y_attn, w_gate, w_proj, out):
                             ident_f[:],
                         )
                 xg = xgp.tile([P, 1024], BF16, name="xg", align_bytes=64)
+                xgs.append(xg)
                 dst = xg[:].bitcast(F32).rearrange("p (m u) -> p m u", u=2)
                 src = ps[:].rearrange("p u m -> p m u")
-                if g % 2 == 0:
-                    nc.scalar.copy(out=dst, in_=src)
-                else:
+                if g == 1:
                     nc.vector.tensor_copy(out=dst, in_=src)
+                else:
+                    nc.scalar.copy(out=dst, in_=src)
+            for g in range(NG):
                 nc.vector.quantize_mx(
                     out=xc[:, g, 256 * half:256 * (half + 1)].bitcast(FP8X4),
                     scales=xs[:, g, 256 * half:256 * (half + 1)],
-                    in_=xg[:],
+                    in_=xgs[g][:],
                 )
 
-        def phase1(c):
-            wcod, wsca = wcs[c]
-            yps = []
-            for half in range(2):
-                yp = psy.tile([P, 4, 256], BF16, name="ybank")
-                yps.append(yp)
-                for j in range(4):
-                    for i in range(2):
-                        nc.tensor.transpose(
-                            yp[:, j, P * i:P * (i + 1)],
-                            y_sb[c][:, 2 * half + i, P * j:P * (j + 1)],
-                            ident_b[:],
-                        )
-            hg = hgp.tile([P, 4 * M], BF16, name="hg", align_bytes=64)
-            for half in range(2):
-                sig = sigp.tile([P, 1024], F32, name="sig")
-                for i in range(2):
-                    mt = 2 * half + i
-                    acc = psum.tile([P, 4, P], F32, name="bank")
-                    for j in range(4):
-                        for g in range(NG):
-                            nc.tensor.matmul_mx(
-                                out=acc[:, j, :],
-                                lhsT=wcod[:, g, P * j:P * (j + 1)].bitcast(FP8X4),
-                                lhsT_scale=wsca[:, g, P * j:P * (j + 1)],
-                                rhs=xc[:, g, P * mt:P * (mt + 1)].bitcast(FP8X4),
-                                rhs_scale=xs[:, g, P * mt:P * (mt + 1)],
-                                start=(g == 0),
-                                stop=(g == NG - 1),
-                            )
-                    nc.scalar.activation(
-                        out=sig[:, 512 * i:512 * (i + 1)].rearrange("p (m j) -> p m j", j=4),
-                        in_=acc[:].rearrange("p j m -> p m j"),
-                        func=ACT.Sigmoid,
-                    )
-                nc.vector.tensor_tensor(
-                    out=hg[:, 1024 * half:1024 * (half + 1)].rearrange("p (m j) -> p m j", j=4),
-                    in0=sig[:].rearrange("p (m j) -> p m j", j=4),
-                    in1=yps[half][:].rearrange("p j m -> p m j"),
-                    op=ALU.mult,
-                )
-            nc.vector.quantize_mx(
-                out=hc[:, c, :].bitcast(FP8X4), scales=hs[:, c, :], in_=hg[:]
-            )
-
-        def phase2_pass(c, accs, g):
-            wcod, wsca = wcs[4 + c]
-            for mt in range(MT):
+        def gate_passes(n, banks):
+            g, h = (n // 2) % NG, n % 2
+            wcod, wsca = cods[n]
+            for j in range(4):
+                if g == 0:
+                    banks[4 * h + j] = psum.tile([P, M], F32, name="bank")
                 nc.tensor.matmul_mx(
-                    out=accs[mt][:],
-                    lhsT=hc[:, g, P * mt:P * (mt + 1)].bitcast(FP8X4),
-                    lhsT_scale=hs[:, g, P * mt:P * (mt + 1)],
-                    rhs=wcod[:, g, :].bitcast(FP8X4),
-                    rhs_scale=wsca[:, g, :],
+                    out=banks[4 * h + j][:],
+                    lhsT=wcod[:, P * j:P * (j + 1)].bitcast(FP8X4),
+                    lhsT_scale=wsca[:, P * j:P * (j + 1)],
+                    rhs=xc[:, g, :].bitcast(FP8X4),
+                    rhs_scale=xs[:, g, :],
                     start=(g == 0),
                     stop=(g == NG - 1),
                 )
 
-        def phase2_out(c, accs):
+        def out_passes(n, banks):
+            g, h = (n // 2) % NG, n % 2
+            wcod, wsca = cods[n]
             for mt in range(MT):
-                ob = outp.tile([P, CH], F32, name="ob")
-                if mt % 2 == 0:
-                    nc.scalar.copy(out=ob[:], in_=accs[mt][:])
-                else:
-                    nc.vector.tensor_copy(out=ob[:], in_=accs[mt][:])
-                nc.sync.dma_start(
-                    out=of[P * mt:P * (mt + 1), CH * c:CH * (c + 1)], in_=ob[:]
+                if g == 0:
+                    banks[4 * h + mt] = psum.tile([P, M], F32, name="bank")
+                nc.tensor.matmul_mx(
+                    out=banks[4 * h + mt][:],
+                    lhsT=hc[:, g, P * mt:P * (mt + 1)].bitcast(FP8X4),
+                    lhsT_scale=hs[:, g, P * mt:P * (mt + 1)],
+                    rhs=wcod[:].bitcast(FP8X4),
+                    rhs_scale=wsca[:],
+                    start=(g == 0),
+                    stop=(g == NG - 1),
                 )
 
-        regroup(0)
-        x_stage(0)
-        regroup(1)
-        quantise(0)
-        x_stage(1)
-        regroup(2)
-        quantise(1)
-        regroup(3)
-        quantise(2)
-        quantise(3)
-        for c in range(NCH):
-            if c + 1 < NCH:
-                for g in range(NG):
-                    regroup(4 * (c + 1) + g)
-                    if g > 0:
-                        quantise(4 * (c + 1) + g - 1)
-                quantise(4 * (c + 1) + 3)
-            phase1(c)
-        for c in range(NCH):
-            accs = [psum.tile([P, CH], F32, name="bank") for mt in range(MT)]
-            for g in range(NG):
-                regroup(16 + 4 * c + g)
-                if g > 0:
-                    quantise(16 + 4 * c + g - 1)
-                    phase2_pass(c, accs, g - 1)
-            quantise(16 + 4 * c + 3)
-            phase2_pass(c, accs, 3)
-            phase2_out(c, accs)
+        sigs = {}
+        yps = {}
+        hgs = {}
+
+        def sigmoids(r, h, banks):
+            sig = sigp.tile([P, 4, M], F32, name="sig")
+            sigs[(r, h)] = sig
+            for j in range(4):
+                nc.scalar.activation(out=sig[:, j, :], in_=banks[4 * h + j][:], func=ACT.Sigmoid)
+
+        def y_transposes(r, h):
+            for half in range(2):
+                yp = psum.tile([P, 4, 256], BF16, name="bank")
+                yps[(r, h, half)] = yp
+                for j in range(4):
+                    for i in range(2):
+                        nc.tensor.transpose(
+                            yp[:, j, P * i:P * (i + 1)],
+                            y_sb[r][:, 2 * half + i, CH * h + P * j:CH * h + P * (j + 1)],
+                            ident_b[:],
+                        )
+
+        def multiply(r, h):
+            hg = hgp.tile([P, 4 * M], BF16, name="hg", align_bytes=64)
+            hgs[(r, h)] = hg
+            for half in range(2):
+                nc.vector.tensor_tensor(
+                    out=hg[:, 1024 * half:1024 * (half + 1)].rearrange("p (m j) -> p m j", j=4),
+                    in0=sigs[(r, h)][:, :, 256 * half:256 * (half + 1)].rearrange("p j m -> p m j"),
+                    in1=yps[(r, h, half)][:].rearrange("p j m -> p m j"),
+                    op=ALU.mult,
+                )
+
+        def quantise_h(r, h):
+            nc.vector.quantize_mx(
+                out=hc[:, 2 * r + h, :].bitcast(FP8X4), scales=hs[:, 2 * r + h, :], in_=hgs[(r, h)][:]
+            )
+
+        def evacuate(c, banks, mt):
+            ob = outp.tile([P, CH], F32, name="ob")
+            src = banks[4 * (c % 2) + mt]
+            if mt in V_EVAC:
+                nc.vector.tensor_copy(out=ob[:], in_=src[:])
+            else:
+                nc.scalar.copy(out=ob[:], in_=src[:])
+            nc.sync.dma_start(out=of[P * mt:P * (mt + 1), CH * c:CH * (c + 1)], in_=ob[:])
+
+        order = [2 * i + h for i in range(8) for h in range(2)]
+        for r in range(2):
+            if ORDER2[r] == "k":
+                order += [16 + 8 * r + 2 * g + h for g in range(NG) for h in range(2)]
+            else:
+                order += [16 + 8 * r + 2 * g + h for h in range(2) for g in range(NG)]
+        pairs = [(order[2 * p], order[2 * p + 1]) for p in range(16)]
+        all_banks = {0: {}, 1: {}, 2: {}, 3: {}}
+        needs = {8: ("sig", 0), 9: ("mul", 0), 16: ("sig", 1), 17: ("mul", 1), 24: ("out", 0), 25: ("out", 1)}
+        held = []
+        done = set()
+        todo = {}
+
+        def flush():
+            while held:
+                n = held[0]
+                if n in needs and needs[n] not in done:
+                    return
+                held.pop(0)
+                (gate_passes if n < 16 else out_passes)(n, all_banks[n // 8])
+
+        def later(p, what):
+            todo[p] = todo.get(p, []) + [what]
+
+        def quantise_and_pass(n, p):
+            quantise(n)
+            held.append(n)
+            flush()
+            if (n // 2) % NG == NG - 1:
+                if n in (7, 15):
+                    later(p + 1 + LAG_S[n // 8], ("sig", n // 8))
+                    later(p + 1 + LAG_V[n // 8], ("mul", n // 8))
+                if n >= 16:
+                    later(p + 1 + LAG_E, ("out", 2 * (n // 8 - 2) + n % 2))
+
+        def empty(c):
+            for mt in range(MT):
+                evacuate(c, all_banks[2 + c // 2], mt)
+            done.add(("out", c))
+            flush()
+
+        for p in range(16):
+            a, b = pairs[p]
+            jobs = todo.get(p, [])
+            for kind, arg in jobs:
+                if kind == "sig":
+                    prev = all_banks[arg]
+                    sigmoids(arg, 0, prev)
+                    y_transposes(arg, 0)
+                    sigmoids(arg, 1, prev)
+                    y_transposes(arg, 1)
+                    done.add(("sig", arg))
+                    flush()
+                if kind == "mul":
+                    multiply(arg, 0)
+                if kind == "out":
+                    empty(arg)
+            regroup(a, "s" if p in S_BOTH else "v")
+            regroup(b, "v" if p in V_BOTH else "s")
+            if p == 0:
+                x_stage(0)
+                x_stage(1)
+            for kind, arg in jobs:
+                if kind == "mul":
+                    quantise_h(arg, 0)
+                    multiply(arg, 1)
+                    done.add(("mul", arg))
+                    flush()
+            if p > 0 and pairs[p - 1][1] not in cods:
+                quantise_and_pass(pairs[p - 1][1], p)
+            quantise_and_pass(a, p)
+            if (b // 2) % NG == NG - 1:
+                quantise_and_pass(b, p)
+            for kind, arg in jobs:
+                if kind == "mul":
+                    quantise_h(arg, 1)
+        for p in sorted(todo):
+            if p >= 16:
+                for kind, arg in todo[p]:
+                    empty(arg)

@@ -21,15 +21,19 @@ MT = M // P
 
 FLOPS = 2 * 2 * M * C * C
 
-NB_RAW = 9
-S_BOTH = ()
-LAG_S = (0, 1)
-LAG_V = (1, 2)
-ORDER2 = ("k", "c")
-V_BOTH = ()
+N_NARROW = 4
+NB_G = 8
+NB_P = 6
+CV = (240, 112, 272, 208, 352, 352, 480, 352, 224, 224, 224, 224, 224, 224, 224, 224, 176, 240, 240, 272, 48, 240, 240, 240, 368, 368, 368, 368, 320, 320, 320, 320)
+LAG_S = 3
+LAG_V = 3
 LAG_E = 2
-V_EVAC = (2, 3)
-Y_AFTER = (4, 8)
+LAG_Y = 0
+V_EVAC = ()
+V_EVAC_LAST = (1, 3)
+X_AFTER = 0
+Y_AT = 3
+X_ON_V = (1,)
 
 
 def tile_multiheadattention_pb_kernel(tc, x, y_attn, w_gate, w_proj, out):
@@ -41,14 +45,16 @@ def tile_multiheadattention_pb_kernel(tc, x, y_attn, w_gate, w_proj, out):
     with ExitStack() as ctx:
         const = ctx.enter_context(tc.tile_pool(name="const", bufs=1))
         keep = ctx.enter_context(tc.tile_pool(name="keep", bufs=1))
-        rawp = ctx.enter_context(tc.tile_pool(name="rawp", bufs=NB_RAW))
-        grpp = ctx.enter_context(tc.tile_pool(name="grpp", bufs=6))
+        rawg = ctx.enter_context(tc.tile_pool(name="rawg", bufs=NB_G))
+        rawq = ctx.enter_context(tc.tile_pool(name="rawq", bufs=NB_P))
+        grpp = ctx.enter_context(tc.tile_pool(name="grpp", bufs=5))
         xgp = ctx.enter_context(tc.tile_pool(name="xgp", bufs=4))
         wcp = ctx.enter_context(tc.tile_pool(name="wcp", bufs=8))
-        sigp = ctx.enter_context(tc.tile_pool(name="sigp", bufs=3))
+        sigp = ctx.enter_context(tc.tile_pool(name="sigp", bufs=2))
         hgp = ctx.enter_context(tc.tile_pool(name="hgp", bufs=2))
         outp = ctx.enter_context(tc.tile_pool(name="outp", bufs=8))
-        psum = ctx.enter_context(tc.psum_pool(name="psum", bufs=8))
+        psum = ctx.enter_context(tc.psum_pool(name="psum", bufs=6))
+        psy = ctx.enter_context(tc.psum_pool(name="psy", bufs=2))
 
         ctx.enter_context(tc.manual_schedule())
 
@@ -58,7 +64,7 @@ def tile_multiheadattention_pb_kernel(tc, x, y_attn, w_gate, w_proj, out):
         make_identity(nc, ident_b[:])
 
         x_sb = [keep.tile([P, C], BF16, name="x_sb%d" % mt) for mt in range(MT)]
-        y_sb = [keep.tile([P, MT, LW], BF16, name="y_sb%d" % r) for r in range(2)]
+        y_sb = [keep.tile([P, MT, CH], BF16, name="y_sb%d" % c) for c in range(4)]
         xc = keep.tile([P, NG, M], U32, name="xc", align_bytes=64)
         xs = keep.tile([P, NG, M], U8, name="xs", align_bytes=64)
         hc = keep.tile([P, NG, M], U32, name="hc", align_bytes=64)
@@ -69,61 +75,99 @@ def tile_multiheadattention_pb_kernel(tc, x, y_attn, w_gate, w_proj, out):
         def load_x(mt):
             nc.sync.dma_start(out=x_sb[mt][:], in_=xf[P * mt:P * (mt + 1), :])
 
-        def load_y(r):
+        def load_y(c):
             nc.sync.dma_start(
-                out=y_sb[r][:],
-                in_=yf[:, LW * r:LW * (r + 1)].rearrange("(t p) c -> p t c", p=P),
+                out=y_sb[c][:],
+                in_=yf[:, CH * c:CH * (c + 1)].rearrange("(t p) c -> p t c", p=P),
             )
 
-        def load_unit(i):
-            raw = rawp.tile([P, 4, LW], BF16, name="raw")
-            raws[i] = raw
-            r, g = (i // NG) % 2, i % NG
-            cols = slice(LW * r, LW * (r + 1))
-            if i < 8:
-                for u in range(2):
-                    r0 = 512 * g + 256 * u
-                    nc.sync.dma_start(
-                        out=raw[:, 2 * u:2 * u + 2, :],
-                        in_=w_gate[r0:r0 + 256, cols].rearrange("(q e) c -> q e c", e=2),
-                    )
-            else:
+        def load_gate(c, g, wide):
+            w = LW if wide else CH
+            raw = (rawq if wide else rawg).tile([P, 4, w], BF16, name="rawq" if wide else "rawg")
+            raws[("g", c, g)] = raw
+            for u in range(2):
+                r0 = 512 * g + 256 * u
                 nc.sync.dma_start(
-                    out=raw[:],
-                    in_=w_proj[512 * g:512 * (g + 1), cols].rearrange("(j p) c -> p j c", p=P),
+                    out=raw[:, 2 * u:2 * u + 2, :],
+                    in_=w_gate[r0:r0 + 256, CH * c:CH * c + w].rearrange("(q e) c -> q e c", e=2),
                 )
 
-        load_unit(0)
-        for mt in range(MT):
-            load_x(mt)
-        for i in range(1, NB_RAW):
-            load_unit(i)
-            if i in Y_AFTER:
-                load_y(Y_AFTER.index(i))
+        def load_proj(c, g):
+            raw = rawq.tile([P, 4, LW], BF16, name="rawq")
+            raws[("p", c, g)] = raw
+            nc.sync.dma_start(
+                out=raw[:],
+                in_=w_proj[512 * g:512 * (g + 1), CH * c:CH * c + LW].rearrange("(j p) c -> p j c", p=P),
+            )
+
+        plan = []
+        items = []
+        for c in range(4):
+            wide = c >= N_NARROW
+            for g in range(NG):
+                if not wide:
+                    plan.append(("n", ("g", c, g)))
+                    items.append((("g", c, g), 0))
+                elif (c - N_NARROW) % 2 == 0:
+                    plan.append(("w", ("g", c, g)))
+                    items.append((("g", c, g), 0))
+                else:
+                    items.append((("g", c - 1, g), CH))
+                if NG * c + g == X_AFTER:
+                    plan += [("x", mt) for mt in range(MT)]
+                if g == Y_AT:
+                    plan.append(("y", c))
+        for c in range(4):
+            for g in range(NG):
+                if c % 2 == 0:
+                    plan.append(("w", ("p", c, g)))
+                items.append((("p", c - c % 2, g), CH * (c % 2)))
+        room = {"n": NB_G, "w": NB_P, "x": MT, "y": 4}
+
+        def load_more():
+            while plan and room[plan[0][0]] > 0:
+                kind, arg = plan.pop(0)
+                room[kind] -= 1
+                if kind == "x":
+                    load_x(arg)
+                elif kind == "y":
+                    load_y(arg)
+                elif arg[0] == "g":
+                    load_gate(arg[1], arg[2], kind == "w")
+                else:
+                    load_proj(arg[1], arg[2])
+
+        load_more()
 
         grps = {}
         cods = {}
-        done_units = {}
+        uses = {}
 
-        def regroup(n, eng):
-            i, h = n // 2, n % 2
-            grp = grpp.tile([P, 4 * CH], BF16, name="grp", align_bytes=64)
-            grps[n] = grp
-            dst = grp[:].rearrange("p (c i t) -> p c t i", i=4, t=4)
-            src = raws[i][:, :, CH * h:CH * (h + 1)].rearrange("p t (c i) -> p c t i", i=4)
-            if eng == "v":
-                nc.vector.tensor_copy(out=dst, in_=src)
-            else:
-                nc.scalar.copy(out=dst, in_=src)
-            done_units[i] = done_units.get(i, 0) + 1
-            if done_units[i] == 2 and i + NB_RAW < 16:
-                load_unit(i + NB_RAW)
+        def regroup(k):
+            i, c0 = items[k]
+            w = CH
+            grp = grpp.tile([P, 4 * w], BF16, name="grp", align_bytes=64)
+            grps[k] = grp
+            cv = CV[k]
+            for eng, a, b in (("v", 0, cv), ("s", cv, w)):
+                if b > a:
+                    dst = grp[:, 4 * a:4 * b].rearrange("p (c i t) -> p c t i", i=4, t=4)
+                    src = raws[i][:, :, c0 + a:c0 + b].rearrange("p t (c i) -> p c t i", i=4)
+                    if eng == "v":
+                        nc.vector.tensor_copy(out=dst, in_=src)
+                    else:
+                        nc.scalar.copy(out=dst, in_=src)
+            uses[i] = uses.get(i, 0) + w
+            if uses[i] == raws[i].shape[2]:
+                room["n" if uses[i] == CH else "w"] += 1
+            load_more()
 
-        def quantise(n):
-            wcod = wcp.tile([P, CH], U32, name="wcod", align_bytes=64)
-            wsca = wcp.tile([P, CH], U8, name="wsca", align_bytes=64)
-            cods[n] = (wcod, wsca)
-            nc.vector.quantize_mx(out=wcod[:].bitcast(FP8X4), scales=wsca[:], in_=grps[n][:])
+        def quantise(k):
+            w = CH
+            wcod = wcp.tile([P, w], U32, name="wcod", align_bytes=64)
+            wsca = wcp.tile([P, w], U8, name="wsca", align_bytes=64)
+            cods[k] = (wcod, wsca)
+            nc.vector.quantize_mx(out=wcod[:].bitcast(FP8X4), scales=wsca[:], in_=grps[k][:])
 
         def x_stage(half):
             xgs = []
@@ -141,7 +185,7 @@ def tile_multiheadattention_pb_kernel(tc, x, y_attn, w_gate, w_proj, out):
                 xgs.append(xg)
                 dst = xg[:].bitcast(F32).rearrange("p (m u) -> p m u", u=2)
                 src = ps[:].rearrange("p u m -> p m u")
-                if g == 1:
+                if g in X_ON_V:
                     nc.vector.tensor_copy(out=dst, in_=src)
                 else:
                     nc.scalar.copy(out=dst, in_=src)
@@ -152,162 +196,155 @@ def tile_multiheadattention_pb_kernel(tc, x, y_attn, w_gate, w_proj, out):
                     in_=xgs[g][:],
                 )
 
-        def gate_passes(n, banks):
-            g, h = (n // 2) % NG, n % 2
-            wcod, wsca = cods[n]
-            for j in range(4):
-                if g == 0:
-                    banks[4 * h + j] = psum.tile([P, M], F32, name="bank")
-                nc.tensor.matmul_mx(
-                    out=banks[4 * h + j][:],
-                    lhsT=wcod[:, P * j:P * (j + 1)].bitcast(FP8X4),
-                    lhsT_scale=wsca[:, P * j:P * (j + 1)],
-                    rhs=xc[:, g, :].bitcast(FP8X4),
-                    rhs_scale=xs[:, g, :],
-                    start=(g == 0),
-                    stop=(g == NG - 1),
-                )
+        banks = {}
 
-        def out_passes(n, banks):
-            g, h = (n // 2) % NG, n % 2
-            wcod, wsca = cods[n]
-            for mt in range(MT):
+        def passes(k):
+            g = k % NG
+            chunk = k // NG
+            wcod, wsca = cods[k]
+            for b in range(4):
                 if g == 0:
-                    banks[4 * h + mt] = psum.tile([P, M], F32, name="bank")
-                nc.tensor.matmul_mx(
-                    out=banks[4 * h + mt][:],
-                    lhsT=hc[:, g, P * mt:P * (mt + 1)].bitcast(FP8X4),
-                    lhsT_scale=hs[:, g, P * mt:P * (mt + 1)],
-                    rhs=wcod[:].bitcast(FP8X4),
-                    rhs_scale=wsca[:],
-                    start=(g == 0),
-                    stop=(g == NG - 1),
-                )
+                    banks[(chunk, b)] = psum.tile([P, M], F32, name="bank")
+                if k < 16:
+                    nc.tensor.matmul_mx(
+                        out=banks[(chunk, b)][:],
+                        lhsT=wcod[:, P * b:P * (b + 1)].bitcast(FP8X4),
+                        lhsT_scale=wsca[:, P * b:P * (b + 1)],
+                        rhs=xc[:, g, :].bitcast(FP8X4),
+                        rhs_scale=xs[:, g, :],
+                        start=(g == 0),
+                        stop=(g == NG - 1),
+                    )
+                else:
+                    nc.tensor.matmul_mx(
+                        out=banks[(chunk, b)][:],
+                        lhsT=hc[:, g, P * b:P * (b + 1)].bitcast(FP8X4),
+                        lhsT_scale=hs[:, g, P * b:P * (b + 1)],
+                        rhs=wcod[:].bitcast(FP8X4),
+                        rhs_scale=wsca[:],
+                        start=(g == 0),
+                        stop=(g == NG - 1),
+                    )
 
         sigs = {}
         yps = {}
         hgs = {}
 
-        def sigmoids(r, h, banks):
+        def sigmoids(c):
             sig = sigp.tile([P, 4, M], F32, name="sig")
-            sigs[(r, h)] = sig
+            sigs[c] = sig
             for j in range(4):
-                nc.scalar.activation(out=sig[:, j, :], in_=banks[4 * h + j][:], func=ACT.Sigmoid)
+                nc.scalar.activation(out=sig[:, j, :], in_=banks[(c, j)][:], func=ACT.Sigmoid)
 
-        def y_transposes(r, h):
+        def y_transposes(c):
             for half in range(2):
-                yp = psum.tile([P, 4, 256], BF16, name="bank")
-                yps[(r, h, half)] = yp
+                yp = psy.tile([P, 4, 256], BF16, name="ybank")
+                yps[(c, half)] = yp
                 for j in range(4):
                     for i in range(2):
                         nc.tensor.transpose(
                             yp[:, j, P * i:P * (i + 1)],
-                            y_sb[r][:, 2 * half + i, CH * h + P * j:CH * h + P * (j + 1)],
+                            y_sb[c][:, 2 * half + i, P * j:P * (j + 1)],
                             ident_b[:],
                         )
 
-        def multiply(r, h):
+        def multiply(c):
             hg = hgp.tile([P, 4 * M], BF16, name="hg", align_bytes=64)
-            hgs[(r, h)] = hg
+            hgs[c] = hg
             for half in range(2):
                 nc.vector.tensor_tensor(
                     out=hg[:, 1024 * half:1024 * (half + 1)].rearrange("p (m j) -> p m j", j=4),
-                    in0=sigs[(r, h)][:, :, 256 * half:256 * (half + 1)].rearrange("p j m -> p m j"),
-                    in1=yps[(r, h, half)][:].rearrange("p j m -> p m j"),
+                    in0=sigs[c][:, :, 256 * half:256 * (half + 1)].rearrange("p j m -> p m j"),
+                    in1=yps[(c, half)][:].rearrange("p j m -> p m j"),
                     op=ALU.mult,
                 )
 
-        def quantise_h(r, h):
-            nc.vector.quantize_mx(
-                out=hc[:, 2 * r + h, :].bitcast(FP8X4), scales=hs[:, 2 * r + h, :], in_=hgs[(r, h)][:]
-            )
+        def quantise_h(c):
+            nc.vector.quantize_mx(out=hc[:, c, :].bitcast(FP8X4), scales=hs[:, c, :], in_=hgs[c][:])
 
-        def evacuate(c, banks, mt):
-            ob = outp.tile([P, CH], F32, name="ob")
-            src = banks[4 * (c % 2) + mt]
-            if mt in V_EVAC:
-                nc.vector.tensor_copy(out=ob[:], in_=src[:])
-            else:
-                nc.scalar.copy(out=ob[:], in_=src[:])
-            nc.sync.dma_start(out=of[P * mt:P * (mt + 1), CH * c:CH * (c + 1)], in_=ob[:])
+        def empty(c, on_v):
+            for mt in range(MT):
+                ob = outp.tile([P, CH], F32, name="ob")
+                if mt in on_v:
+                    nc.vector.tensor_copy(out=ob[:], in_=banks[(4 + c, mt)][:])
+                else:
+                    nc.scalar.copy(out=ob[:], in_=banks[(4 + c, mt)][:])
+                nc.sync.dma_start(out=of[P * mt:P * (mt + 1), CH * c:CH * (c + 1)], in_=ob[:])
 
-        order = [2 * i + h for i in range(8) for h in range(2)]
-        for r in range(2):
-            if ORDER2[r] == "k":
-                order += [16 + 8 * r + 2 * g + h for g in range(NG) for h in range(2)]
-            else:
-                order += [16 + 8 * r + 2 * g + h for h in range(2) for g in range(NG)]
-        pairs = [(order[2 * p], order[2 * p + 1]) for p in range(16)]
-        all_banks = {0: {}, 1: {}, 2: {}, 3: {}}
-        needs = {8: ("sig", 0), 9: ("mul", 0), 16: ("sig", 1), 17: ("mul", 1), 24: ("out", 0), 25: ("out", 1)}
+        NI = len(items)
         held = []
         done = set()
         todo = {}
 
+        def need(k):
+            wants = [("x", 0)]
+            if k >= 16:
+                wants.append(("hq", k % NG))
+            if k % NG == 0 and k > 0:
+                wants.append(("sig", k // NG - 1) if k <= 16 else ("out", k // NG - 5))
+            return wants
+
         def flush():
             while held:
-                n = held[0]
-                if n in needs and needs[n] not in done:
+                k = held[0]
+                if not all(w in done for w in need(k)):
                     return
                 held.pop(0)
-                (gate_passes if n < 16 else out_passes)(n, all_banks[n // 8])
+                passes(k)
 
-        def later(p, what):
-            todo[p] = todo.get(p, []) + [what]
+        def later(k, what):
+            todo[k] = todo.get(k, []) + [what]
 
-        def quantise_and_pass(n, p):
-            quantise(n)
-            held.append(n)
+        def quantise_and_pass(k, now):
+            quantise(k)
+            held.append(k)
             flush()
-            if (n // 2) % NG == NG - 1:
-                if n in (7, 15):
-                    later(p + 1 + LAG_S[n // 8], ("sig", n // 8))
-                    later(p + 1 + LAG_V[n // 8], ("mul", n // 8))
-                if n >= 16:
-                    later(p + 1 + LAG_E, ("out", 2 * (n // 8 - 2) + n % 2))
+            if k % NG == NG - 1:
+                if k < 16:
+                    later(now + 1 + LAG_S, ("sig", k // NG))
+                    later(now + 1 + LAG_V, ("mul", k // NG))
+                    if k < 12:
+                        later(now + 2 + LAG_V + LAG_Y, ("ytr", k // NG + 1))
+                else:
+                    later(now + 1 + LAG_E, ("out", k // NG - 4))
 
-        def empty(c):
-            for mt in range(MT):
-                evacuate(c, all_banks[2 + c // 2], mt)
-            done.add(("out", c))
-            flush()
+        def run_job(kind, arg, stage):
+            if kind == "ytr" and stage == 0:
+                y_transposes(arg)
+            if kind == "sig" and stage == 0:
+                sigmoids(arg)
+                done.add(("sig", arg))
+                flush()
+            if kind == "mul" and stage == 0:
+                multiply(arg)
+            if kind == "mul" and stage == 2:
+                quantise_h(arg)
+                done.add(("hq", arg))
+                flush()
+            if kind == "out" and stage == 0:
+                empty(arg, V_EVAC_LAST if arg == 3 else V_EVAC)
+                done.add(("out", arg))
+                flush()
 
-        for p in range(16):
-            a, b = pairs[p]
-            jobs = todo.get(p, [])
+        later(2, ("ytr", 0))
+        for k in range(NI):
+            jobs = todo.get(k, [])
             for kind, arg in jobs:
-                if kind == "sig":
-                    prev = all_banks[arg]
-                    sigmoids(arg, 0, prev)
-                    y_transposes(arg, 0)
-                    sigmoids(arg, 1, prev)
-                    y_transposes(arg, 1)
-                    done.add(("sig", arg))
-                    flush()
-                if kind == "mul":
-                    multiply(arg, 0)
-                if kind == "out":
-                    empty(arg)
-            regroup(a, "s" if p in S_BOTH else "v")
-            regroup(b, "v" if p in V_BOTH else "s")
-            if p == 0:
+                run_job(kind, arg, 0)
+            regroup(k)
+            if k == X_AFTER:
                 x_stage(0)
                 x_stage(1)
+                done.add(("x", 0))
+                flush()
+            if k > 0 and (k - 1) not in cods:
+                quantise_and_pass(k - 1, k)
+            if k == NI - 1:
+                quantise_and_pass(k, k)
             for kind, arg in jobs:
-                if kind == "mul":
-                    quantise_h(arg, 0)
-                    multiply(arg, 1)
-                    done.add(("mul", arg))
-                    flush()
-            if p > 0 and pairs[p - 1][1] not in cods:
-                quantise_and_pass(pairs[p - 1][1], p)
-            quantise_and_pass(a, p)
-            if (b // 2) % NG == NG - 1:
-                quantise_and_pass(b, p)
-            for kind, arg in jobs:
-                if kind == "mul":
-                    quantise_h(arg, 1)
-        for p in sorted(todo):
-            if p >= 16:
-                for kind, arg in todo[p]:
-                    empty(arg)
+                run_job(kind, arg, 2)
+        for k in sorted(todo):
+            if k >= NI:
+                for kind, arg in todo[k]:
+                    for stage in range(3):
+                        run_job(kind, arg, stage)

@@ -21,19 +21,21 @@ MT = M // P
 
 FLOPS = 2 * 2 * M * C * C
 
+OUT_CHUNKS = ((0, 512), (512, 512), (1024, 512), (1536, 256), (1792, 256))
 N_NARROW = 4
 NB_G = 8
 NB_P = 6
-CV = (240, 112, 272, 208, 352, 352, 480, 352, 224, 224, 224, 224, 224, 224, 224, 224, 176, 240, 240, 272, 48, 240, 240, 240, 368, 368, 368, 368, 320, 320, 320, 320)
-LAG_S = 3
-LAG_V = 3
-LAG_E = 2
+CV = (256, 128, 224, 224, 352, 352, 512, 320, 224, 224, 224, 224, 224, 224, 224, 224, 176, 240, 240, 272, 48, 240, 240, 240, 368, 368, 368, 368, 160, 160, 160, 160, 160, 160, 128, 160)
+LAG_S = (1, 3, 3, 3)
+LAG_V = (3, 3, 3, 3)
+LAG_E = (3, 2, 4, 3, 0)
 LAG_Y = 0
 V_EVAC = ()
 V_EVAC_LAST = (1, 3)
-X_AFTER = 0
+X_AFTER = 1
+X_GAP = 0
 Y_AT = 3
-X_ON_V = (1,)
+X_ON_V = ()
 
 
 def tile_multiheadattention_pb_kernel(tc, x, y_attn, w_gate, w_proj, out):
@@ -107,21 +109,22 @@ def tile_multiheadattention_pb_kernel(tc, x, y_attn, w_gate, w_proj, out):
             for g in range(NG):
                 if not wide:
                     plan.append(("n", ("g", c, g)))
-                    items.append((("g", c, g), 0))
+                    items.append((("g", c, g), 0, CH))
                 elif (c - N_NARROW) % 2 == 0:
                     plan.append(("w", ("g", c, g)))
-                    items.append((("g", c, g), 0))
+                    items.append((("g", c, g), 0, CH))
                 else:
-                    items.append((("g", c - 1, g), CH))
+                    items.append((("g", c - 1, g), CH, CH))
                 if NG * c + g == X_AFTER:
                     plan += [("x", mt) for mt in range(MT)]
                 if g == Y_AT:
                     plan.append(("y", c))
-        for c in range(4):
+        for c in (0, 2):
             for g in range(NG):
-                if c % 2 == 0:
-                    plan.append(("w", ("p", c, g)))
-                items.append((("p", c - c % 2, g), CH * (c % 2)))
+                plan.append(("w", ("p", c, g)))
+        for lo, w in OUT_CHUNKS:
+            for g in range(NG):
+                items.append((("p", 2 * (lo // LW), g), lo % LW, w))
         room = {"n": NB_G, "w": NB_P, "x": MT, "y": 4}
 
         def load_more():
@@ -144,8 +147,7 @@ def tile_multiheadattention_pb_kernel(tc, x, y_attn, w_gate, w_proj, out):
         uses = {}
 
         def regroup(k):
-            i, c0 = items[k]
-            w = CH
+            i, c0, w = items[k]
             grp = grpp.tile([P, 4 * w], BF16, name="grp", align_bytes=64)
             grps[k] = grp
             cv = CV[k]
@@ -163,7 +165,7 @@ def tile_multiheadattention_pb_kernel(tc, x, y_attn, w_gate, w_proj, out):
             load_more()
 
         def quantise(k):
-            w = CH
+            w = items[k][2]
             wcod = wcp.tile([P, w], U32, name="wcod", align_bytes=64)
             wsca = wcp.tile([P, w], U8, name="wsca", align_bytes=64)
             cods[k] = (wcod, wsca)
@@ -203,8 +205,10 @@ def tile_multiheadattention_pb_kernel(tc, x, y_attn, w_gate, w_proj, out):
             chunk = k // NG
             wcod, wsca = cods[k]
             for b in range(4):
-                if g == 0:
-                    banks[(chunk, b)] = psum.tile([P, M], F32, name="bank")
+                if g == 0 and k >= 16 and b == 3:
+                    banks[(chunk, b)] = psy.tile([P, items[k][2]], F32, name="ybank")
+                elif g == 0:
+                    banks[(chunk, b)] = psum.tile([P, items[k][2]], F32, name="bank")
                 if k < 16:
                     nc.tensor.matmul_mx(
                         out=banks[(chunk, b)][:],
@@ -263,13 +267,14 @@ def tile_multiheadattention_pb_kernel(tc, x, y_attn, w_gate, w_proj, out):
             nc.vector.quantize_mx(out=hc[:, c, :].bitcast(FP8X4), scales=hs[:, c, :], in_=hgs[c][:])
 
         def empty(c, on_v):
+            lo, w = OUT_CHUNKS[c]
             for mt in range(MT):
-                ob = outp.tile([P, CH], F32, name="ob")
+                ob = outp.tile([P, w], F32, name="ob")
                 if mt in on_v:
                     nc.vector.tensor_copy(out=ob[:], in_=banks[(4 + c, mt)][:])
                 else:
                     nc.scalar.copy(out=ob[:], in_=banks[(4 + c, mt)][:])
-                nc.sync.dma_start(out=of[P * mt:P * (mt + 1), CH * c:CH * (c + 1)], in_=ob[:])
+                nc.sync.dma_start(out=of[P * mt:P * (mt + 1), lo:lo + w], in_=ob[:])
 
         NI = len(items)
         held = []
@@ -281,7 +286,12 @@ def tile_multiheadattention_pb_kernel(tc, x, y_attn, w_gate, w_proj, out):
             if k >= 16:
                 wants.append(("hq", k % NG))
             if k % NG == 0 and k > 0:
-                wants.append(("sig", k // NG - 1) if k <= 16 else ("out", k // NG - 5))
+                if k < 16:
+                    wants.append(("sig", k // NG - 1))
+                elif k < 24:
+                    wants += [("sig", 3), ("hq", 3)]
+                else:
+                    wants.append(("out", k // NG - 6))
             return wants
 
         def flush():
@@ -301,12 +311,12 @@ def tile_multiheadattention_pb_kernel(tc, x, y_attn, w_gate, w_proj, out):
             flush()
             if k % NG == NG - 1:
                 if k < 16:
-                    later(now + 1 + LAG_S, ("sig", k // NG))
-                    later(now + 1 + LAG_V, ("mul", k // NG))
+                    later(now + 1 + LAG_S[k // NG], ("sig", k // NG))
+                    later(now + 1 + LAG_V[k // NG], ("mul", k // NG))
                     if k < 12:
-                        later(now + 2 + LAG_V + LAG_Y, ("ytr", k // NG + 1))
+                        later(now + 2 + LAG_V[k // NG] + LAG_Y, ("ytr", k // NG + 1))
                 else:
-                    later(now + 1 + LAG_E, ("out", k // NG - 4))
+                    later(now + 1 + LAG_E[k // NG - 4], ("out", k // NG - 4))
 
         def run_job(kind, arg, stage):
             if kind == "ytr" and stage == 0:
@@ -322,7 +332,7 @@ def tile_multiheadattention_pb_kernel(tc, x, y_attn, w_gate, w_proj, out):
                 done.add(("hq", arg))
                 flush()
             if kind == "out" and stage == 0:
-                empty(arg, V_EVAC_LAST if arg == 3 else V_EVAC)
+                empty(arg, V_EVAC_LAST if arg == len(OUT_CHUNKS) - 1 else V_EVAC)
                 done.add(("out", arg))
                 flush()
 
@@ -332,13 +342,15 @@ def tile_multiheadattention_pb_kernel(tc, x, y_attn, w_gate, w_proj, out):
             for kind, arg in jobs:
                 run_job(kind, arg, 0)
             regroup(k)
+            if k > 0 and (k - 1) not in cods:
+                quantise_and_pass(k - 1, k)
             if k == X_AFTER:
+                quantise_and_pass(k, k)
                 x_stage(0)
+            if k == X_AFTER + X_GAP:
                 x_stage(1)
                 done.add(("x", 0))
                 flush()
-            if k > 0 and (k - 1) not in cods:
-                quantise_and_pass(k - 1, k)
             if k == NI - 1:
                 quantise_and_pass(k, k)
             for kind, arg in jobs:

@@ -60,6 +60,11 @@ def tile_multiheadattention_pb_kernel(tc, x, y_attn, w_gate, w_proj, out):
 
         ctx.enter_context(tc.manual_schedule())
 
+        warm_in = const.tile([P, 1], F32, name="warm_in")
+        warm_out = const.tile([P, 1], F32, name="warm_out")
+        nc.vector.memset(warm_in[:], 0.0)
+        nc.scalar.activation(out=warm_out[:], in_=warm_in[:], func=ACT.Sigmoid)
+
         ident_f = const.tile([P, P], F32, name="ident_f")
         make_identity(nc, ident_f[:])
         ident_b = const.tile([P, P], BF16, name="ident_b")

@@ -55,13 +55,14 @@ def tile_multiheadattention_pb_kernel(tc, x, y_attn, w_gate, w_proj, out):
         sigp = ctx.enter_context(tc.tile_pool(name="sigp", bufs=2))
         hgp = ctx.enter_context(tc.tile_pool(name="hgp", bufs=2))
         outp = ctx.enter_context(tc.tile_pool(name="outp", bufs=8))
+        warmp = ctx.enter_context(tc.tile_pool(name="warmp", bufs=1))
         psum = ctx.enter_context(tc.psum_pool(name="psum", bufs=6))
         psy = ctx.enter_context(tc.psum_pool(name="psy", bufs=2))
 
         ctx.enter_context(tc.manual_schedule())
 
-        warm_in = const.tile([P, 1], F32, name="warm_in")
-        warm_out = const.tile([P, 1], F32, name="warm_out")
+        warm_in = warmp.tile([P, 1], F32, name="warm_in")
+        warm_out = warmp.tile([P, 1], F32, name="warm_out")
         nc.vector.memset(warm_in[:], 0.0)
         nc.scalar.activation(out=warm_out[:], in_=warm_in[:], func=ACT.Sigmoid)
 

@@ -59,8 +59,6 @@ def tile_multiheadattention_pb_kernel(tc, x, y_attn, w_gate, w_proj, out):
         psum = ctx.enter_context(tc.psum_pool(name="psum", bufs=6))
         psy = ctx.enter_context(tc.psum_pool(name="psy", bufs=2))
 
-        ctx.enter_context(tc.manual_schedule())
-
         warm_in = warmp.tile([P, 1], F32, name="warm_in")
         warm_out = warmp.tile([P, 1], F32, name="warm_out")
         nc.vector.memset(warm_in[:], 0.0)

@@ -25,16 +25,17 @@ OUT_CHUNKS = ((0, 512), (512, 512), (1024, 512), (1536, 256), (1792, 256))
 N_NARROW = 4
 NB_G = 8
 NB_P = 6
-CV = (256, 128, 224, 224, 352, 352, 512, 320, 224, 224, 224, 224, 224, 224, 224, 224, 176, 240, 240, 272, 48, 240, 240, 240, 368, 368, 368, 368, 160, 160, 160, 160, 160, 160, 128, 160)
-LAG_S = (1, 3, 3, 3)
-LAG_V = (3, 3, 3, 3)
-LAG_E = (3, 2, 4, 3, 0)
-LAG_Y = 0
+CV = (512, 320, 320, 224, 272, 304, 512, 288, 320, 240, 192, 240, 288, 80, 304, 288, 192, 112, 384, 192, 0, 272, 272, 336, 432, 384, 192, 432, 240, 96, 176, 128, 176, 128, 160, 176)
+LAG_S = (1, 3, 3, 1)
+LAG_V = (4, 3, 5, 4)
+LAG_E = (3, 3, 4, 5, 5)
+LAG_Y = 1
 V_EVAC = ()
-V_EVAC_LAST = (1, 3)
-X_AFTER = 1
+V_EVAC_LAST = (2, 3)
+X_AFTER = 2
+YTR0 = 5
 X_GAP = 0
-Y_AT = 3
+Y_AT = 7
 X_ON_V = ()
 
 
@@ -58,6 +59,8 @@ def tile_multiheadattention_pb_kernel(tc, x, y_attn, w_gate, w_proj, out):
         warmp = ctx.enter_context(tc.tile_pool(name="warmp", bufs=1))
         psum = ctx.enter_context(tc.psum_pool(name="psum", bufs=6))
         psy = ctx.enter_context(tc.psum_pool(name="psy", bufs=2))
+
+        ctx.enter_context(tc.manual_schedule())
 
         warm_in = warmp.tile([P, 1], F32, name="warm_in")
         warm_out = warmp.tile([P, 1], F32, name="warm_out")
@@ -121,11 +124,13 @@ def tile_multiheadattention_pb_kernel(tc, x, y_attn, w_gate, w_proj, out):
                     items.append((("g", c - 1, g), CH, CH))
                 if NG * c + g == X_AFTER:
                     plan += [("x", mt) for mt in range(MT)]
-                if g == Y_AT:
-                    plan.append(("y", c))
+                if NG * c + g >= Y_AT and (NG * c + g - Y_AT) % NG == 0:
+                    plan.append(("y", (NG * c + g - Y_AT) // NG))
         for c in (0, 2):
             for g in range(NG):
                 plan.append(("w", ("p", c, g)))
+                if c == 0 and 16 + g >= Y_AT and (16 + g - Y_AT) % NG == 0:
+                    plan.append(("y", (16 + g - Y_AT) // NG))
         for lo, w in OUT_CHUNKS:
             for g in range(NG):
                 items.append((("p", 2 * (lo // LW), g), lo % LW, w))
@@ -340,7 +345,7 @@ def tile_multiheadattention_pb_kernel(tc, x, y_attn, w_gate, w_proj, out):
                 done.add(("out", arg))
                 flush()
 
-        later(2, ("ytr", 0))
+        later(YTR0, ("ytr", 0))
         for k in range(NI):
             jobs = todo.get(k, [])
             for kind, arg in jobs:

from contextlib import ExitStack

import concourse.mybir as mybir
from concourse.masks import make_identity

F32 = mybir.dt.float32
BF16 = mybir.dt.bfloat16
U32 = mybir.dt.uint32
U8 = mybir.dt.uint8
FP8X4 = mybir.dt.float8_e4m3fn_x4
ACT = mybir.ActivationFunctionType
ALU = mybir.AluOpType

P = 128
M = 512
C = 2048
NG = 4
LW = 1024
CH = 512
MT = M // P

FLOPS = 2 * 2 * M * C * C

OUT_CHUNKS = ((0, 512), (512, 512), (1024, 512), (1536, 256), (1792, 256))
N_NARROW = 4
NB_G = 8
NB_P = 6
CV = (512, 320, 320, 224, 272, 304, 512, 288, 320, 240, 192, 240, 288, 80, 304, 288, 192, 112, 384, 192, 0, 272, 272, 336, 432, 384, 192, 432, 240, 96, 176, 128, 176, 128, 160, 176)
LAG_S = (1, 3, 3, 1)
LAG_V = (4, 3, 5, 4)
LAG_E = (3, 3, 4, 5, 5)
LAG_Y = 1
V_EVAC = ()
V_EVAC_LAST = (2, 3)
X_AFTER = 2
YTR0 = 5
X_GAP = 0
Y_AT = 7
X_ON_V = ()


def tile_multiheadattention_pb_kernel(tc, x, y_attn, w_gate, w_proj, out):
    nc = tc.nc
    xf = x.flatten_outer_dims()
    yf = y_attn.rearrange("b t h d -> (b t) (h d)")
    of = out.flatten_outer_dims()

    with ExitStack() as ctx:
        const = ctx.enter_context(tc.tile_pool(name="const", bufs=1))
        keep = ctx.enter_context(tc.tile_pool(name="keep", bufs=1))
        rawg = ctx.enter_context(tc.tile_pool(name="rawg", bufs=NB_G))
        rawq = ctx.enter_context(tc.tile_pool(name="rawq", bufs=NB_P))
        grpp = ctx.enter_context(tc.tile_pool(name="grpp", bufs=5))
        xgp = ctx.enter_context(tc.tile_pool(name="xgp", bufs=4))
        wcp = ctx.enter_context(tc.tile_pool(name="wcp", bufs=8))
        sigp = ctx.enter_context(tc.tile_pool(name="sigp", bufs=2))
        hgp = ctx.enter_context(tc.tile_pool(name="hgp", bufs=2))
        outp = ctx.enter_context(tc.tile_pool(name="outp", bufs=8))
        warmp = ctx.enter_context(tc.tile_pool(name="warmp", bufs=1))
        psum = ctx.enter_context(tc.psum_pool(name="psum", bufs=6))
        psy = ctx.enter_context(tc.psum_pool(name="psy", bufs=2))

        ctx.enter_context(tc.manual_schedule())

        warm_in = warmp.tile([P, 1], F32, name="warm_in")
        warm_out = warmp.tile([P, 1], F32, name="warm_out")
        nc.vector.memset(warm_in[:], 0.0)
        nc.scalar.activation(out=warm_out[:], in_=warm_in[:], func=ACT.Sigmoid)

        ident_f = const.tile([P, P], F32, name="ident_f")
        make_identity(nc, ident_f[:])
        ident_b = const.tile([P, P], BF16, name="ident_b")
        make_identity(nc, ident_b[:])

        x_sb = [keep.tile([P, C], BF16, name="x_sb%d" % mt) for mt in range(MT)]
        y_sb = [keep.tile([P, MT, CH], BF16, name="y_sb%d" % c) for c in range(4)]
        xc = keep.tile([P, NG, M], U32, name="xc", align_bytes=64)
        xs = keep.tile([P, NG, M], U8, name="xs", align_bytes=64)
        hc = keep.tile([P, NG, M], U32, name="hc", align_bytes=64)
        hs = keep.tile([P, NG, M], U8, name="hs", align_bytes=64)

        raws = {}

        def load_x(mt):
            nc.sync.dma_start(out=x_sb[mt][:], in_=xf[P * mt:P * (mt + 1), :])

        def load_y(c):
            nc.sync.dma_start(
                out=y_sb[c][:],
                in_=yf[:, CH * c:CH * (c + 1)].rearrange("(t p) c -> p t c", p=P),
            )

        def load_gate(c, g, wide):
            w = LW if wide else CH
            raw = (rawq if wide else rawg).tile([P, 4, w], BF16, name="rawq" if wide else "rawg")
            raws[("g", c, g)] = raw
            for u in range(2):
                r0 = 512 * g + 256 * u
                nc.sync.dma_start(
                    out=raw[:, 2 * u:2 * u + 2, :],
                    in_=w_gate[r0:r0 + 256, CH * c:CH * c + w].rearrange("(q e) c -> q e c", e=2),
                )

        def load_proj(c, g):
            raw = rawq.tile([P, 4, LW], BF16, name="rawq")
            raws[("p", c, g)] = raw
            nc.sync.dma_start(
                out=raw[:],
                in_=w_proj[512 * g:512 * (g + 1), CH * c:CH * c + LW].rearrange("(j p) c -> p j c", p=P),
            )

        plan = []
        items = []
        for c in range(4):
            wide = c >= N_NARROW
            for g in range(NG):
                if not wide:
                    plan.append(("n", ("g", c, g)))
                    items.append((("g", c, g), 0, CH))
                elif (c - N_NARROW) % 2 == 0:
                    plan.append(("w", ("g", c, g)))
                    items.append((("g", c, g), 0, CH))
                else:
                    items.append((("g", c - 1, g), CH, CH))
                if NG * c + g == X_AFTER:
                    plan += [("x", mt) for mt in range(MT)]
                if NG * c + g >= Y_AT and (NG * c + g - Y_AT) % NG == 0:
                    plan.append(("y", (NG * c + g - Y_AT) // NG))
        for c in (0, 2):
            for g in range(NG):
                plan.append(("w", ("p", c, g)))
                if c == 0 and 16 + g >= Y_AT and (16 + g - Y_AT) % NG == 0:
                    plan.append(("y", (16 + g - Y_AT) // NG))
        for lo, w in OUT_CHUNKS:
            for g in range(NG):
                items.append((("p", 2 * (lo // LW), g), lo % LW, w))
        room = {"n": NB_G, "w": NB_P, "x": MT, "y": 4}

        def load_more():
            while plan and room[plan[0][0]] > 0:
                kind, arg = plan.pop(0)
                room[kind] -= 1
                if kind == "x":
                    load_x(arg)
                elif kind == "y":
                    load_y(arg)
                elif arg[0] == "g":
                    load_gate(arg[1], arg[2], kind == "w")
                else:
                    load_proj(arg[1], arg[2])

        load_more()

        grps = {}
        cods = {}
        uses = {}

        def regroup(k):
            i, c0, w = items[k]
            grp = grpp.tile([P, 4 * w], BF16, name="grp", align_bytes=64)
            grps[k] = grp
            cv = CV[k]
            for eng, a, b in (("v", 0, cv), ("s", cv, w)):
                if b > a:
                    dst = grp[:, 4 * a:4 * b].rearrange("p (c i t) -> p c t i", i=4, t=4)
                    src = raws[i][:, :, c0 + a:c0 + b].rearrange("p t (c i) -> p c t i", i=4)
                    if eng == "v":
                        nc.vector.tensor_copy(out=dst, in_=src)
                    else:
                        nc.scalar.copy(out=dst, in_=src)
            uses[i] = uses.get(i, 0) + w
            if uses[i] == raws[i].shape[2]:
                room["n" if uses[i] == CH else "w"] += 1
            load_more()

        def quantise(k):
            w = items[k][2]
            wcod = wcp.tile([P, w], U32, name="wcod", align_bytes=64)
            wsca = wcp.tile([P, w], U8, name="wsca", align_bytes=64)
            cods[k] = (wcod, wsca)
            nc.vector.quantize_mx(out=wcod[:].bitcast(FP8X4), scales=wsca[:], in_=grps[k][:])

        def x_stage(half):
            xgs = []
            for g in range(NG):
                ps = psum.tile([P, 2, 256], F32, name="bank")
                for u in range(2):
                    for i in range(2):
                        w0 = 256 * g + 128 * u
                        nc.tensor.transpose(
                            ps[:, u, P * i:P * (i + 1)],
                            x_sb[2 * half + i][:].bitcast(F32)[:, w0:w0 + P],
                            ident_f[:],
                        )
                xg = xgp.tile([P, 1024], BF16, name="xg", align_bytes=64)
                xgs.append(xg)
                dst = xg[:].bitcast(F32).rearrange("p (m u) -> p m u", u=2)
                src = ps[:].rearrange("p u m -> p m u")
                if g in X_ON_V:
                    nc.vector.tensor_copy(out=dst, in_=src)
                else:
                    nc.scalar.copy(out=dst, in_=src)
            for g in range(NG):
                nc.vector.quantize_mx(
                    out=xc[:, g, 256 * half:256 * (half + 1)].bitcast(FP8X4),
                    scales=xs[:, g, 256 * half:256 * (half + 1)],
                    in_=xgs[g][:],
                )

        banks = {}

        def passes(k):
            g = k % NG
            chunk = k // NG
            wcod, wsca = cods[k]
            for b in range(4):
                if g == 0 and k >= 16 and b == 3:
                    banks[(chunk, b)] = psy.tile([P, items[k][2]], F32, name="ybank")
                elif g == 0:
                    banks[(chunk, b)] = psum.tile([P, items[k][2]], F32, name="bank")
                if k < 16:
                    nc.tensor.matmul_mx(
                        out=banks[(chunk, b)][:],
                        lhsT=wcod[:, P * b:P * (b + 1)].bitcast(FP8X4),
                        lhsT_scale=wsca[:, P * b:P * (b + 1)],
                        rhs=xc[:, g, :].bitcast(FP8X4),
                        rhs_scale=xs[:, g, :],
                        start=(g == 0),
                        stop=(g == NG - 1),
                    )
                else:
                    nc.tensor.matmul_mx(
                        out=banks[(chunk, b)][:],
                        lhsT=hc[:, g, P * b:P * (b + 1)].bitcast(FP8X4),
                        lhsT_scale=hs[:, g, P * b:P * (b + 1)],
                        rhs=wcod[:].bitcast(FP8X4),
                        rhs_scale=wsca[:],
                        start=(g == 0),
                        stop=(g == NG - 1),
                    )

        sigs = {}
        yps = {}
        hgs = {}

        def sigmoids(c):
            sig = sigp.tile([P, 4, M], F32, name="sig")
            sigs[c] = sig
            for j in range(4):
                nc.scalar.activation(out=sig[:, j, :], in_=banks[(c, j)][:], func=ACT.Sigmoid)

        def y_transposes(c):
            for half in range(2):
                yp = psy.tile([P, 4, 256], BF16, name="ybank")
                yps[(c, half)] = yp
                for j in range(4):
                    for i in range(2):
                        nc.tensor.transpose(
                            yp[:, j, P * i:P * (i + 1)],
                            y_sb[c][:, 2 * half + i, P * j:P * (j + 1)],
                            ident_b[:],
                        )

        def multiply(c):
            hg = hgp.tile([P, 4 * M], BF16, name="hg", align_bytes=64)
            hgs[c] = hg
            for half in range(2):
                nc.vector.tensor_tensor(
                    out=hg[:, 1024 * half:1024 * (half + 1)].rearrange("p (m j) -> p m j", j=4),
                    in0=sigs[c][:, :, 256 * half:256 * (half + 1)].rearrange("p j m -> p m j"),
                    in1=yps[(c, half)][:].rearrange("p j m -> p m j"),
                    op=ALU.mult,
                )

        def quantise_h(c):
            nc.vector.quantize_mx(out=hc[:, c, :].bitcast(FP8X4), scales=hs[:, c, :], in_=hgs[c][:])

        def empty(c, on_v):
            lo, w = OUT_CHUNKS[c]
            for mt in range(MT):
                ob = outp.tile([P, w], F32, name="ob")
                if mt in on_v:
                    nc.vector.tensor_copy(out=ob[:], in_=banks[(4 + c, mt)][:])
                else:
                    nc.scalar.copy(out=ob[:], in_=banks[(4 + c, mt)][:])
                nc.sync.dma_start(out=of[P * mt:P * (mt + 1), lo:lo + w], in_=ob[:])

        NI = len(items)
        held = []
        done = set()
        todo = {}

        def need(k):
            wants = [("x", 0)]
            if k >= 16:
                wants.append(("hq", k % NG))
            if k % NG == 0 and k > 0:
                if k < 16:
                    wants.append(("sig", k // NG - 1))
                elif k < 24:
                    wants += [("sig", 3), ("hq", 3)]
                else:
                    wants.append(("out", k // NG - 6))
            return wants

        def flush():
            while held:
                k = held[0]
                if not all(w in done for w in need(k)):
                    return
                held.pop(0)
                passes(k)

        def later(k, what):
            todo[k] = todo.get(k, []) + [what]

        def quantise_and_pass(k, now):
            quantise(k)
            held.append(k)
            flush()
            if k % NG == NG - 1:
                if k < 16:
                    later(now + 1 + LAG_S[k // NG], ("sig", k // NG))
                    later(now + 1 + LAG_V[k // NG], ("mul", k // NG))
                    if k < 12:
                        later(now + 2 + LAG_V[k // NG] + LAG_Y, ("ytr", k // NG + 1))
                else:
                    later(now + 1 + LAG_E[k // NG - 4], ("out", k // NG - 4))

        def run_job(kind, arg, stage):
            if kind == "ytr" and stage == 0:
                y_transposes(arg)
            if kind == "sig" and stage == 0:
                sigmoids(arg)
                done.add(("sig", arg))
                flush()
            if kind == "mul" and stage == 0:
                multiply(arg)
            if kind == "mul" and stage == 2:
                quantise_h(arg)
                done.add(("hq", arg))
                flush()
            if kind == "out" and stage == 0:
                empty(arg, V_EVAC_LAST if arg == len(OUT_CHUNKS) - 1 else V_EVAC)
                done.add(("out", arg))
                flush()

        later(YTR0, ("ytr", 0))
        for k in range(NI):
            jobs = todo.get(k, [])
            for kind, arg in jobs:
                run_job(kind, arg, 0)
            regroup(k)
            if k > 0 and (k - 1) not in cods:
                quantise_and_pass(k - 1, k)
            if k == X_AFTER:
                quantise_and_pass(k, k)
                x_stage(0)
            if k == X_AFTER + X_GAP:
                x_stage(1)
                done.add(("x", 0))
                flush()
            if k == NI - 1:
                quantise_and_pass(k, k)
            for kind, arg in jobs:
                run_job(kind, arg, 2)
        for k in sorted(todo):
            if k >= NI:
                for kind, arg in todo[k]:
                    for stage in range(3):
                        run_job(kind, arg, stage)
